import numpy as np
import ml_dtypes


def mxq(x, axis, fmt="e4m3"):
    dtype, down = {"e4m3": (ml_dtypes.float8_e4m3fn, 7), "e5m2": (ml_dtypes.float8_e5m2, 14)}[fmt]
    v = np.moveaxis(np.asarray(x, np.float32).astype(ml_dtypes.bfloat16).astype(np.float64), axis, -1)
    blocks = v.reshape(v.shape[:-1] + (-1, 32))
    amax = np.abs(blocks).max(-1, keepdims=True)
    byte = np.maximum(np.where(amax > 0, np.frexp(amax)[1] - 1 + 127, 0) - down, 1)
    scale = np.exp2(byte - 127.0)
    codes = (blocks / scale).astype(np.float32).astype(dtype).astype(np.float64)
    return np.moveaxis((codes * scale).reshape(v.shape), -1, axis)


WIDE = False


def mx_kscale(k):
    if not WIDE:
        return np.ones(k)
    levels = np.array([18, -18])
    if k % 512:
        return np.exp2(np.random.permutation(np.resize(levels, k // 32))).repeat(32)
    a = np.empty((k // 512, 16))
    for p in range(k // 512):
        a[p, :8] = np.random.permutation(np.resize(levels, 8))
        for g in range(8):
            far = levels[np.abs(levels - a[p, g]) >= 10]
            a[p, g + 8] = far[np.random.randint(len(far))]
    return np.exp2(a.ravel()).repeat(32)


BF16 = ml_dtypes.bfloat16


def bf(x):
    return np.asarray(x, np.float32).astype(BF16)


def f64(x):
    return np.asarray(x).astype(np.float64)


B, CIN, COUT, E = 2048, 512, 512, 4
OMEGA_0 = 30.0


def gated_sum(in_feats, tile_gate, W):
    x, g, w = f64(in_feats), f64(tile_gate), f64(W)
    acc = np.zeros((B, COUT))
    for t in range(E):
        acc = acc + g[:, t:t + 1] * (x @ w[t].T)
    return acc


def setup_inputs():
    s = mx_kscale(B)[:, None]
    u = mx_kscale(E * COUT).reshape(E, COUT)
    v = u[:, 0]
    c = u[0] / u[0, 0]
    wb = np.sqrt(6.0 / CIN) / OMEGA_0
    x0 = bf(np.random.standard_normal((B, CIN)))
    g0 = bf(np.random.standard_normal((B, E)) / np.sqrt(E))
    w0 = bf(np.random.uniform(-wb, wb, (E, COUT, CIN)))
    go = bf(np.random.standard_normal((B, COUT)) * np.exp2(np.random.randint(-6, 1, (B, 1))) * 0.25 / s * c)
    acc = gated_sum(x0, g0, w0)
    return {"in_feats": bf(f64(x0) * s),
            "tile_gate": bf(f64(g0) * v),
            "W": bf(f64(w0) / (v[:, None, None] * c[None, :, None])),
            "acc": np.asarray(acc, np.float32),
            "grad_out": go}


def reference(in_feats, tile_gate, W, acc, grad_out):
    dacc = f64(grad_out) * (OMEGA_0 * np.cos(OMEGA_0 * f64(acc)))
    dz = (f64(tile_gate)[:, :, None] * dacc[:, None, :]).reshape(B, E * COUT)
    wf = f64(W).reshape(E * COUT, CIN)
    dx = mxq(dz, 1, "e5m2") @ mxq(wf, 0, "e4m3")
    dw = mxq(dz, 0, "e5m2").T @ mxq(f64(in_feats), 0, "e4m3")
    return dx, dw.reshape(E, COUT, CIN)

import math
from contextlib import ExitStack

import concourse.mybir as mybir
from concourse.masks import make_identity

B, CIN, COUT, E = 2048, 512, 512, 4
OMEGA_0 = 30.0
FLOPS = 2 * 2 * B * E * COUT * CIN

F32 = mybir.dt.float32
BF16 = mybir.dt.bfloat16
I32 = mybir.dt.int32
U32 = mybir.dt.uint32
U8 = mybir.dt.uint8
E4M3 = mybir.dt.float8_e4m3fn_x4
E5M2 = mybir.dt.float8_e5m2_x4
ALU = mybir.AluOpType
ACT = mybir.ActivationFunctionType

P = 128
G = B // (4 * P)
BANKS = {"T": 2, "O": 2, "P": 4}
TURNS = OMEGA_0 / (2.0 * math.pi)


SCALAR_ROWS = (2, 4, 3, 2, 3, 4, 1, 3, 2, 0, 2, 1, 0, 0, 4, 3)
SCALAR_COPIES = (0, 0, 0, 0, 0, 0, 0, 0, 0, 0, 1, 0, 0, 1, 0, 0)


def scalar_rows(n):
    return tuple(range(4 - SCALAR_ROWS[n], 4))


def tile_sinelayer_loe_pa_v_kernel(tc, in_feats, tile_gate, W, acc, grad_out, out_0, out_1):
    nc = tc.nc
    acc_v = acc.rearrange("(g p j) w -> g p j w", p=P, j=4)
    go_v = grad_out.rearrange("(g p j) w -> g p j w", p=P, j=4)
    x_v = in_feats.rearrange("(g p j) c -> g p j c", p=P, j=4)
    w_v = W.rearrange("t (p j) c -> t p j c", j=4)
    gate_v = tile_gate.rearrange("(g p j) t -> p g (j t)", p=P, j=4)
    out0_v = out_0.rearrange("(g p j) c -> g j p c", p=P, j=4)
    out1_v = out_1.rearrange("t (q m) c -> t m q c", m=4)

    with ExitStack() as ctx:
        sb = ctx.enter_context(tc.tile_pool(name="sb", bufs=1))
        ps = ctx.enter_context(tc.psum_pool(name="ps", bufs=1))

        ident_f = sb.tile([P, P], F32, name="ident_f")
        ident_b = sb.tile([P, P], BF16, name="ident_b")
        make_identity(nc, ident_b[:])
        make_identity(nc, ident_f[:])

        with tc.manual_schedule():
            gate_raw = sb.tile([P, G, 16], BF16, name="gate_raw")
            gate30 = sb.tile([P, G * 16], F32, name="gate30")
            warm = sb.tile([P, 1], F32, name="warm")

            acc_t, go_t, raw_t = {}, {}, {}

            def load_acc(g, h):
                a = sb.tile([P, 2, COUT], F32, name="acc_t", tag="acc", bufs=8)
                nc.sync.dma_start(out=a[:], in_=acc_v[g, :, 2 * h:2 * h + 2, :])
                acc_t[g, h] = a

            def load_go(g, h):
                a = sb.tile([P, 2, COUT], BF16, name="go_t", tag="go", bufs=8)
                nc.sync.dma_start(out=a[:], in_=go_v[g, :, 2 * h:2 * h + 2, :])
                go_t[g, h] = a

            def load_raw(i):
                a = sb.tile([P, 4, CIN], BF16, name="raw_t", tag="raw", bufs=8)
                nc.sync.dma_start(out=a[:], in_=(w_v[i] if i < 4 else x_v[i - 4]))
                raw_t[i] = a

            load_acc(0, 0)
            load_acc(0, 1)
            nc.sync.dma_start(out=gate_raw[:], in_=gate_v)
            load_go(0, 0)
            load_go(0, 1)
            load_raw(0)
            load_acc(1, 0)
            load_acc(1, 1)
            load_raw(1)
            load_go(1, 0)
            load_go(1, 1)
            load_raw(2)
            load_raw(3)
            load_acc(2, 0)
            load_acc(2, 1)
            load_raw(4)
            load_go(2, 0)
            load_go(2, 1)
            load_raw(5)
            load_acc(3, 0)
            load_acc(3, 1)
            load_go(3, 0)
            load_go(3, 1)
            load_raw(6)
            load_raw(7)

            nc.vector.memset(warm[:], 0.0)
            nc.scalar.activation(out=warm[:], in_=warm[:], func=ACT.Sin)

            dacc_t, dz_t, dzi_t, dzt_t = {}, {}, {}, {}
            c1, s1, c2, s2, cw, sw = {}, {}, {}, {}, {}, {}
            rawi_t, pb, ob = {}, {}, {}

            def reduce_angle(g, h):
                a = acc_t[g, h][:].rearrange("p j w -> p (j w)")
                k = sb.tile([P, 2 * COUT], I32, name="k", tag="k", bufs=2)
                nc.vector.tensor_scalar(out=k[:], in0=a, scalar1=TURNS, scalar2=0.25, op0=ALU.mult, op1=ALU.add)
                return k

            def subtract_turns(g, h, k):
                a = acc_t[g, h][:].rearrange("p j w -> p (j w)")
                nc.vector.scalar_tensor_tensor(out=a, in0=a, scalar=TURNS, in1=k[:], op0=ALU.mult, op1=ALU.subtract)

            def sine(g, h):
                a = acc_t[g, h][:].rearrange("p j w -> p (j w)")
                nc.scalar.activation(out=a, in_=a, func=ACT.Sin, bias=0.5 * math.pi, scale=2.0 * math.pi)

            def make_dacc(g, h):
                d = sb.tile([P, 2, 256, 2], F32, name="dacc", tag="dacc", bufs=4)
                nc.vector.tensor_tensor(
                    out=d[:],
                    in0=acc_t[g, h][:].rearrange("p j (q u e) -> p u (j q) e", u=2, e=2),
                    in1=go_t[g, h][:].rearrange("p j (q u e) -> p u (j q) e", u=2, e=2),
                    op=ALU.mult,
                )
                dacc_t[g, h] = d

            def gate_rows(n, js, scalar):
                g, t = divmod(n, 4)
                if n not in dz_t:
                    dz_t[n] = sb.tile([P, 4, 2, 256], BF16, name="dz", tag="dz", bufs=3)
                for j in js:
                    src = dacc_t[g, j // 2][:].rearrange("p u (j q) e -> p j u (q e)", j=2)[:, j % 2]
                    dst = dz_t[n][:, j]
                    col = 16 * g + 4 * j + t
                    if scalar:
                        nc.scalar.activation(out=dst, in_=src, func=ACT.Copy, scale=gate30[:, col:col + 1])
                    else:
                        nc.vector.tensor_scalar(out=dst, in0=src, scalar1=gate30[:, col:col + 1], scalar2=None, op0=ALU.mult)

            def make_dz(n):
                js = scalar_rows(n)
                gate_rows(n, [j for j in range(4) if j not in js], False)
                gate_rows(n, js, True)

            def transposes(n):
                words = dz_t[n][:].rearrange("p j u w -> p (j u w)").bitcast(F32)
                banks = []
                for b in range(2):
                    x = ps.tile([P, 4, P], F32, name="xt", tag="T", bufs=2)
                    for i in range(4):
                        w0 = (4 * b + i) * P
                        nc.tensor.transpose(x[:, i, :], words[:, w0:w0 + P], ident_f[:])
                    banks.append(x)
                return banks

            def copy_transposed(n, banks):
                d = sb.tile([P, 4, P, 4], BF16, name="dzt", tag="dzt", bufs=2)
                dzt_t[n] = d
                words = d[:].rearrange("p j i k -> p (j i k)").bitcast(F32)
                for b in range(2):
                    nc.scalar.copy(
                        out=words[:, 512 * b:512 * (b + 1)].rearrange("p (j i u) -> p j i u", j=2, u=2),
                        in_=banks[b][:].rearrange("p (j u) i -> p j i u", u=2),
                    )

            def quantize_features(n):
                c = sb.tile([P, 512], U32, name="c2", tag="c2", bufs=8, align_bytes=64)
                s = sb.tile([P, 512], U8, name="s2", tag="s2", bufs=8, align_bytes=64)
                nc.vector.quantize_mx(out=c[:].bitcast(E5M2), scales=s[:], in_=dzt_t[n][:].rearrange("p j i k -> p (j i k)"))
                c2[n], s2[n] = c, s

            def interleave(n, u, scalar=False):
                if u == 0:
                    dzi_t[n] = sb.tile([P, 2, 2, P, 4], BF16, name="dzi", tag="dzi", bufs=2, align_bytes=64)
                copy = nc.scalar.copy if scalar else nc.vector.tensor_copy
                copy(
                    out=dzi_t[n][:, u],
                    in_=dz_t[n][:].rearrange("p j u (q e) -> p u e q j", e=2)[:, u],
                )

            def quantize_tokens(n):
                c = sb.tile([P, 512], U32, name="c1_%d" % n, align_bytes=64)
                s = sb.tile([P, 512], U8, name="s1_%d" % n, align_bytes=64)
                nc.vector.quantize_mx(out=c[:].bitcast(E5M2), scales=s[:], in_=dzi_t[n][:].rearrange("p u e q j -> p (u e q j)"))
                c1[n], s1[n] = c, s

            def move_raw(i):
                banks = []
                for b in range(2):
                    m = ps.tile([P, 2, P, 4], BF16, name="mv", tag="P", bufs=4)
                    for k in range(2):
                        c0 = (2 * b + k) * P
                        nc.tensor.matmul(
                            m[:, k],
                            lhsT=ident_b[:],
                            rhs=raw_t[i][:].rearrange("p j c -> p c j")[:, c0:c0 + P, :],
                            start=True,
                            stop=True,
                        )
                    banks.append(m)
                return banks

            def copy_raw(i, banks):
                r = sb.tile([P, 2, 1024], BF16, name="rawi", tag="rawi", bufs=2, align_bytes=64)
                rawi_t[i] = r
                for b in range(2):
                    nc.scalar.copy(out=r[:, b, :], in_=banks[b][:].rearrange("p k c j -> p (k c j)"))

            def quantize_raw(i):
                c = sb.tile([P, 512], U32, name="cw_%d" % i, align_bytes=64)
                s = sb.tile([P, 512], U8, name="sw_%d" % i, align_bytes=64)
                nc.vector.quantize_mx(out=c[:].bitcast(E4M3), scales=s[:], in_=rawi_t[i][:].rearrange("p b w -> p (b w)"))
                cw[i], sw[i] = c, s

            def pass_0(g, j, t, tag):
                if t == 0:
                    ob[g, j] = ps.tile([P, CIN], F32, name="o0", tag=tag, bufs=BANKS[tag])
                n = 4 * g + t
                nc.tensor.matmul_mx(
                    out=ob[g, j][:],
                    lhsT=c2[n][:, P * j:P * (j + 1)].bitcast(E5M2),
                    lhsT_scale=s2[n][:, P * j:P * (j + 1)],
                    rhs=cw[t][:].bitcast(E4M3),
                    rhs_scale=sw[t][:],
                    start=(t == 0),
                    stop=(t == 3),
                )

            def store_0(g, j, vector=False):
                r = sb.tile([P, CIN], F32, name="res", tag="res", bufs=6)
                if vector:
                    nc.vector.tensor_copy(out=r[:], in_=ob[g, j][:])
                else:
                    nc.scalar.copy(out=r[:], in_=ob[g, j][:])
                nc.sync.dma_start(out=out0_v[g, j], in_=r[:])

            def pass_1(t, m, g, start, stop, tag):
                if start:
                    pb[t, m] = ps.tile([P, CIN], F32, name="o1", tag=tag, bufs=BANKS[tag])
                n = 4 * g + t
                nc.tensor.matmul_mx(
                    out=pb[t, m][:],
                    lhsT=c1[n][:, P * m:P * (m + 1)].bitcast(E5M2),
                    lhsT_scale=s1[n][:, P * m:P * (m + 1)],
                    rhs=cw[4 + g][:].bitcast(E4M3),
                    rhs_scale=sw[4 + g][:],
                    start=start,
                    stop=stop,
                )

            def park_1(t, m):
                if m % 2 == 0:
                    part_t[t, m // 2] = sb.tile([P, 2, CIN], F32, name="part", tag="raw", bufs=8)
                nc.scalar.copy(out=part_t[t, m // 2][:, m % 2], in_=pb[t, m][:])

            def store_1(t, m, engine):
                r = sb.tile([P, CIN], F32, name="res", tag="res", bufs=6)
                if (t, m // 2) in part_t:
                    nc.vector.tensor_tensor(out=r[:], in0=pb[t, m][:], in1=part_t[t, m // 2][:, m % 2], op=ALU.add)
                elif engine == "V":
                    nc.vector.tensor_copy(out=r[:], in_=pb[t, m][:])
                else:
                    nc.scalar.copy(out=r[:], in_=pb[t, m][:])
                nc.sync.dma_start(out=out1_v[t, m], in_=r[:])

            part_t, kk = {}, {}

            kk[0, 0] = reduce_angle(0, 0)
            kk[0, 1] = reduce_angle(0, 1)
            subtract_turns(0, 0, kk[0, 0])
            sine(0, 0)
            subtract_turns(0, 1, kk[0, 1])
            sine(0, 1)
            nc.vector.tensor_scalar(out=gate30[:], in0=gate_raw[:].rearrange("p g w -> p (g w)"), scalar1=OMEGA_0, scalar2=None, op0=ALU.mult)
            rb = move_raw(0)
            copy_raw(0, rb)
            make_dacc(0, 0)
            make_dacc(0, 1)
            make_dz(0)
            xt = {0: transposes(0)}
            kk[1, 0] = reduce_angle(1, 0)
            quantize_raw(0)
            subtract_turns(1, 0, kk[1, 0])
            make_dz(1)
            sine(1, 0)
            kk[1, 1] = reduce_angle(1, 1)
            subtract_turns(1, 1, kk[1, 1])

            for s in range(17):
                i = s + 1
                done = []
                if s >= 5 and s % 4 in (1, 2):
                    done = [((s - 5) // 4, 2 * ((s - 5) % 4) + h) for h in range(2)]
                for g, j in done[:1]:
                    for t in range(4):
                        pass_0(g, j, t, "O")
                if i < 8:
                    rb = move_raw(i)
                if s < 16:
                    copy_transposed(s, xt[s])
                if s == 16:
                    done = []
                if s in (14, 15, 16):
                    for m in range(2):
                        pass_1(s - 14, m, 2, True, False, "O")
                        pass_1(s - 14, m, 3, False, True, "O")
                if s < 16:
                    interleave(s, 0, SCALAR_COPIES[s] > 1)
                if 1 <= s <= 16:
                    quantize_features(s - 1)
                if s < 16:
                    interleave(s, 1, SCALAR_COPIES[s] > 0)
                for g, j in done[:1]:
                    store_0(g, j)
                if 7 <= s < 10:
                    for m in range(4):
                        park_1(s - 7, m)
                if s + 1 < 16:
                    xt[s + 1] = transposes(s + 1)
                for g, j in done[1:]:
                    for t in range(4):
                        pass_0(g, j, t, "O")
                if s in (14, 15, 16):
                    for m in range(2):
                        store_1(s - 14, m, "V")
                    for m in range(2, 4):
                        pass_1(s - 14, m, 2, True, False, "O")
                        pass_1(s - 14, m, 3, False, True, "O")
                if 6 <= s < 10:
                    for m in range(4):
                        for g in range(2):
                            pass_1(s - 6, m, g, g == 0, g == 1 and s < 9, "P")
                if s == 13:
                    for m in range(4):
                        pass_1(3, m, 2, False, False, "P")
                for g in range(1, 4):
                    for h in range(2):
                        if g > 1 and s == 4 * g - 6 + h:
                            kk[g, h] = reduce_angle(g, h)
                        if s == 4 * g - 4 + h:
                            make_dacc(g, h)
                if 1 <= s <= 16:
                    quantize_tokens(s - 1)
                for g in range(1, 4):
                    for h in range(2):
                        if g > 1 and s == 4 * g - 6 + h:
                            subtract_turns(g, h, kk[g, h])
                        if (g, h) != (1, 0) and s == 4 * g - 5 + h:
                            sine(g, h)
                if s in (14, 15, 16):
                    for m in range(2, 4):
                        store_1(s - 14, m, "V")
                if 1 <= s <= 7:
                    quantize_raw(s)
                if i < 8:
                    copy_raw(i, rb)
                for g, j in done[1:]:
                    store_0(g, j)
                if s + 2 < 16:
                    make_dz(s + 2)
                if s == 15:
                    for j in range(2):
                        for t in range(3):
                            pass_0(3, j, t, "T")
                if s == 16:
                    for m in range(4):
                        pass_1(3, m, 3, False, True, "P")
                    for j in range(2):
                        pass_0(3, j, 3, "T")
                    for j in range(2, 4):
                        for t in range(4):
                            pass_0(3, j, t, "O")
                    for m in range(4):
                        store_1(3, m, "VS"[m % 2])
                    for j in range(4):
                        store_0(3, j, j % 2 == 0)
